import numpy as np
import ml_dtypes


def mxq(x, axis, fmt="e4m3"):
    dtype, down = {"e4m3": (ml_dtypes.float8_e4m3fn, 7), "e5m2": (ml_dtypes.float8_e5m2, 14)}[fmt]
    v = np.moveaxis(np.asarray(x, np.float32).astype(ml_dtypes.bfloat16).astype(np.float64), axis, -1)
    blocks = v.reshape(v.shape[:-1] + (-1, 32))
    amax = np.abs(blocks).max(-1, keepdims=True)
    byte = np.maximum(np.where(amax > 0, np.frexp(amax)[1] - 1 + 127, 0) - down, 1)
    scale = np.exp2(byte - 127.0)
    codes = (blocks / scale).astype(np.float32).astype(dtype).astype(np.float64)
    return np.moveaxis((codes * scale).reshape(v.shape), -1, axis)


WIDE = False


def mx_kscale(k):
    if not WIDE:
        return np.ones(k)
    levels = np.array([10, -10, 5, -5, 0])
    if k % 512:
        return np.exp2(np.random.permutation(np.resize(levels, k // 32))).repeat(32)
    a = np.empty((k // 512, 16))
    for p in range(k // 512):
        a[p, :8] = np.random.permutation(np.resize(levels, 8))
        for g in range(8):
            far = levels[np.abs(levels - a[p, g]) >= 10]
            a[p, g + 8] = far[np.random.randint(len(far))]
    return np.exp2(a.ravel()).repeat(32)


BF16 = ml_dtypes.bfloat16


def bf(x):
    return np.asarray(x, np.float32).astype(BF16)


def f64(x):
    return np.asarray(x).astype(np.float64)


B, S, H, O, W = 8, 2048, 512, 128, 8


def setup_inputs():
    s = mx_kscale(H)
    return {"hidden_states": bf(np.random.standard_normal((B, S, H)) * s),
            "gate_proj": bf(np.random.standard_normal((O, H)) / np.sqrt(H) / s[None, :]),
            "world_size": W}


def core(hidden_states, gate_proj, world_size):
    h = gate_proj.shape[1]
    view = f64(hidden_states).reshape(-1, h)
    mm = mxq(view, 1, "e4m3") @ mxq(f64(gate_proj), 1, "e4m3").T
    n, o = mm.shape
    out = mm.reshape(world_size, n // world_size, o).sum(axis=0)
    return out


def e4m3fn_bytes(y):
    return np.clip(np.asarray(y, np.float64), -448.0, 448.0).astype(np.float32).astype(ml_dtypes.float8_e4m3fn).view(np.uint8)


def reference(hidden_states, gate_proj, world_size):
    out = core(hidden_states, gate_proj, world_size)
    s = np.max(np.abs(out), axis=-1, keepdims=True) / 448.0
    return out, e4m3fn_bytes(out / s)

@@ -1,0 +1,275 @@
+from contextlib import ExitStack
+
+import concourse.mybir as mybir
+from concourse.masks import make_identity
+
+F32 = mybir.dt.float32
+BF16 = mybir.dt.bfloat16
+U32 = mybir.dt.uint32
+U8 = mybir.dt.uint8
+FP8X4 = mybir.dt.float8_e4m3fn_x4
+FP8 = mybir.dt.float8_e4m3fn
+ALU = mybir.AluOpType
+ACT = mybir.ActivationFunctionType
+AX = mybir.AxisListType
+
+R, J, K, O = 8, 2048, 512, 128
+FLOPS = 2 * R * J * K * O
+
+P = 128
+KW = K // 2
+NI = 4
+NJB = J // (P * NI)
+FP8_MAX = 448.0
+RUN = 8
+PRE_LEAD = 2
+
+
+def load_pieces(jb):
+    if jb == 0:
+        return [1, 1, 2, 2, 2]
+    if jb == NJB - 1:
+        return [2, 2, 2, 1, 1]
+    return [2, 2, 2, 2]
+
+
+def unit_plan():
+    units = []
+    runs = []
+    for jb in range(NJB):
+        for r in range(R):
+            if r % 2 == 0:
+                runs.append([])
+            if jb == NJB - 1 and r == R - 1:
+                for i0 in range(0, NI, 2):
+                    runs[-1].append(len(units))
+                    units.append((jb, r, i0, 2, False))
+            else:
+                runs[-1].append(len(units))
+                units.append((jb, r, 0, NI, r % 2 == 1 and (jb, r) != (0, 1)))
+    return units, runs
+
+
+def tile_testmmrsmodel_t_kernel(tc, hidden_states, gate_proj, world_size, out_0, out_1):
+    nc = tc.nc
+    assert world_size == R
+
+    with ExitStack() as ctx:
+        keep = ctx.enter_context(tc.tile_pool(name="keep", bufs=1))
+        ppool = ctx.enter_context(tc.tile_pool(name="ppool", bufs=3))
+        gpool = ctx.enter_context(tc.tile_pool(name="gpool", bufs=4))
+        cpool = ctx.enter_context(tc.tile_pool(name="cpool", bufs=8))
+        opool = ctx.enter_context(tc.tile_pool(name="opool", bufs=NJB))
+        pst = ctx.enter_context(tc.psum_pool(name="pst", bufs=8 - NI))
+        psa = ctx.enter_context(tc.psum_pool(name="psa", bufs=NI))
+        ctx.enter_context(tc.manual_schedule())
+
+        ident = keep.tile([P, P], F32, name="ident")
+        make_identity(nc, ident[:])
+        zero = keep.tile([P, 1], F32, name="zero")
+        nc.gpsimd.memset(zero[:], 0.0)
+        warm = keep.tile([P, 1], F32, name="warm")
+        nc.scalar.activation(out=warm[:], in_=zero[:], func=ACT.Identity, scale=zero[:, 0:1], bias=zero[:, 0:1])
+
+        where = {}
+        gate_sb = keep.tile([P, K], BF16, name="gate_sb")
+        for jb in range(NJB):
+            r0 = 0
+            for nr in load_pieces(jb):
+                x = keep.tile([P, nr * NI * K], BF16, name="x%d_%d" % (jb, r0))
+                nc.sync.dma_start(
+                    out=x[:].rearrange("p (r e) -> p r e", r=nr),
+                    in_=hidden_states[r0 : r0 + nr, jb * P * NI : (jb + 1) * P * NI, :].rearrange(
+                        "r (p i) k -> p r (i k)", i=NI
+                    ),
+                )
+                for rr in range(nr):
+                    where[(jb, r0 + rr)] = (x[:].bitcast(F32), rr * NI * KW)
+                if jb == 0 and r0 == 0:
+                    nc.sync.dma_start(out=gate_sb[:], in_=gate_proj[:, :])
+                r0 += nr
+
+        units, runs = unit_plan()
+        pcs = {}
+        banks = {}
+        quant = {}
+        acc = {}
+        gcodes = keep.tile([P, 2 * O], U32, name="gcodes", align_bytes=64)
+        gscl = keep.tile([P, 2 * O], U8, name="gscl", align_bytes=64)
+        gg = keep.tile([P, 2 * K], BF16, name="gg", align_bytes=64)
+
+        def deinterleave_words(dst, src):
+            nc.vector.tensor_copy(
+                out=dst.rearrange("p u (b i) -> p u b i", i=RUN),
+                in_=src.rearrange("p (b u i) -> p u b i", u=2, i=RUN),
+            )
+
+        def deinterleave(k):
+            if k >= len(units) or not units[k][4]:
+                return
+            jb, r, i0, ni, pre = units[k]
+            words, off = where[(jb, r)]
+            pc = ppool.tile([P, 2, ni * KW // 2], F32, name="pc")
+            deinterleave_words(pc[:], words[:, off + i0 * KW : off + (i0 + ni) * KW])
+            pcs[k] = pc
+
+        def transpose_pair(xt, a, src):
+            for u in range(2):
+                nc.tensor.transpose(xt[:, a, u, :], src(u), ident[:])
+
+        def transposes(k):
+            jb, r, i0, ni, pre = units[k]
+            banks[k] = []
+            for b in range(ni // 2):
+                xt = pst.tile([P, 2, 2, P], F32, name="xt")
+                for a in range(2):
+                    t = 2 * b + a
+                    if pre:
+                        pc = pcs[k]
+                        transpose_pair(xt, a, lambda u: pc[:, u, t * P : (t + 1) * P])
+                    else:
+                        words, off = where[(jb, r)]
+                        lo = off + (i0 + t) * KW
+                        transpose_pair(xt, a, lambda u: words[:, lo + u : lo + KW : 2])
+                banks[k].append(xt)
+
+        def drain(xt, n, dst_words):
+            nc.scalar.copy(
+                out=dst_words.rearrange("p (a r u) -> p a r u", a=n, u=2),
+                in_=xt[:, 0:n, :, :].rearrange("p a u r -> p a r u"),
+            )
+
+        late_stores = []
+
+        def drains_and_quantize(k):
+            jb, r, i0, ni, pre = units[k]
+            g = gpool.tile([P, ni * K], BF16, name="g", align_bytes=64)
+            gw = g[:].bitcast(F32)
+            for b in range(ni // 2):
+                drain(banks[k][b], 2, gw[:, 2 * b * KW : 2 * (b + 1) * KW])
+            if k == len(units) - 2:
+                for rows, o32 in late_stores:
+                    nc.scalar.dma_start(
+                        out=out_0[rows, :].rearrange("(p i) o -> p (i o)", i=NI),
+                        in_=o32[:].rearrange("p i o -> p (i o)"),
+                    )
+            codes = cpool.tile([P, ni * P], U32, name="codes", align_bytes=64)
+            scl = cpool.tile([P, ni * P], U8, name="scl", align_bytes=64)
+            nc.vector.quantize_mx(out=codes[:].bitcast(FP8X4), scales=scl[:], in_=g[:])
+            quant[k] = (codes, scl)
+
+        def matmuls(k):
+            jb, r, i0, ni, pre = units[k]
+            codes, scl = quant[k]
+            gcols = slice(O, 2 * O) if pre else slice(0, O)
+            for t in range(ni):
+                i = i0 + t
+                if r == 0:
+                    acc[i] = psa.tile([P, O], F32, name="acc")
+                cols = slice(t * P, (t + 1) * P)
+                nc.tensor.matmul_mx(
+                    out=acc[i][:],
+                    lhsT=codes[:, cols].bitcast(FP8X4),
+                    lhsT_scale=scl[:, cols],
+                    rhs=gcodes[:, gcols].bitcast(FP8X4),
+                    rhs_scale=gscl[:, gcols],
+                    start=(r == 0),
+                    stop=(r == R - 1),
+                )
+
+        ep = {}
+
+        def epilogue_stage(jb, stage, last):
+            rows = slice(jb * P * NI, (jb + 1) * P * NI)
+            if stage == 0:
+                o32 = opool.tile([P, NI, O], F32, name="o32")
+                for i in range(NI):
+                    if last and i == NI - 1:
+                        nc.vector.tensor_copy(out=o32[:, i, :], in_=acc[i][:])
+                    else:
+                        nc.scalar.copy(out=o32[:, i, :], in_=acc[i][:])
+                if last:
+                    nc.sync.dma_start(
+                        out=out_0[rows, :].rearrange("(p i) o -> p (i o)", i=NI),
+                        in_=o32[:].rearrange("p i o -> p (i o)"),
+                    )
+                else:
+                    late_stores.append((rows, o32))
+                ep[jb] = {"o32": o32}
+            elif stage == 1:
+                amax = opool.tile([P, NI], F32, name="amax")
+                nc.vector.tensor_reduce(
+                    out=amax[:], in_=ep[jb]["o32"][:], axis=AX.X, op=ALU.max, apply_absolute_value=True
+                )
+                ep[jb]["amax"] = amax
+            elif stage == 2:
+                rc = opool.tile([P, NI], F32, name="rc")
+                nc.vector.reciprocal(out=rc[:], in_=ep[jb]["amax"][:])
+                ep[jb]["rc"] = rc
+            elif stage == 3:
+                rs = opool.tile([P, NI], F32, name="rs")
+                nc.vector.tensor_scalar(out=rs[:], in0=ep[jb]["rc"][:], scalar1=FP8_MAX, scalar2=None, op0=ALU.mult)
+                ep[jb]["rs"] = rs
+            else:
+                o8 = opool.tile([P, NI, O], FP8, name="o8")
+                for i in range(NI):
+                    if last and i % 2 == 1:
+                        nc.scalar.activation(
+                            out=o8[:, i, :],
+                            in_=ep[jb]["o32"][:, i, :],
+                            func=ACT.Identity,
+                            scale=ep[jb]["rs"][:, i : i + 1],
+                            bias=zero[:, 0:1],
+                            saturate=False,
+                        )
+                    else:
+                        nc.vector.tensor_scalar(
+                            out=o8[:, i, :],
+                            in0=ep[jb]["o32"][:, i, :],
+                            scalar1=ep[jb]["rs"][:, i : i + 1],
+                            scalar2=None,
+                            op0=ALU.mult,
+                            saturate=False,
+                        )
+                nc.sync.dma_start(
+                    out=out_1[rows, :].rearrange("(p i) o -> p (i o)", i=NI),
+                    in_=o8[:].rearrange("p i o -> p (i o)").bitcast(U8),
+                )
+
+        gpc = keep.tile([P, 2, KW // 2], F32, name="gpc")
+        deinterleave_words(gpc[:], gate_sb[:].bitcast(F32))
+        for k in range(PRE_LEAD):
+            deinterleave(k)
+
+        pending = []
+        for j, run in enumerate(runs):
+            for k in run:
+                deinterleave(k + PRE_LEAD)
+                transposes(k)
+                if k == 0:
+                    gxt = pst.tile([P, 2, 2, P], F32, name="xt")
+                    gwords = gate_sb[:].bitcast(F32)
+                    transpose_pair(gxt, 0, lambda u: gwords[:, u:KW:2])
+                    transpose_pair(gxt, 1, lambda u: gpc[:, u, :])
+                drains_and_quantize(k)
+                if k == 0:
+                    drain(gxt, 2, gg[:].bitcast(F32))
+                if k == 1:
+                    nc.vector.quantize_mx(out=gcodes[:].bitcast(FP8X4), scales=gscl[:], in_=gg[:])
+                for e in pending:
+                    epilogue_stage(e[0], e[1], False)
+                    e[1] += 1
+                pending = [e for e in pending if e[1] < 5]
+            if j >= 1:
+                for k in runs[j - 1]:
+                    matmuls(k)
+                    if units[k][1] == R - 1:
+                        epilogue_stage(units[k][0], 0, False)
+                        pending.append([units[k][0], 1])
+        for k in runs[-1]:
+            matmuls(k)
+        for e in pending:
+            for stage in range(e[1], 5):
+                epilogue_stage(e[0], stage, False)
+        for stage in range(5):
+            epilogue_stage(NJB - 1, stage, True)

@@ -22,7 +22,8 @@ NI = 4
 NJB = J // (P * NI)
 FP8_MAX = 448.0
 RUN = 8
-PRE_LEAD = 2
+PRE_LEAD = 3
+MM_LAG = 2
 
 
 def load_pieces(jb):
@@ -56,9 +57,9 @@ def tile_testmmrsmodel_t_kernel(tc, hidden_states, gate_proj, world_size, out_0,
 
     with ExitStack() as ctx:
         keep = ctx.enter_context(tc.tile_pool(name="keep", bufs=1))
-        ppool = ctx.enter_context(tc.tile_pool(name="ppool", bufs=3))
+        ppool = ctx.enter_context(tc.tile_pool(name="ppool", bufs=PRE_LEAD + 1))
         gpool = ctx.enter_context(tc.tile_pool(name="gpool", bufs=4))
-        cpool = ctx.enter_context(tc.tile_pool(name="cpool", bufs=8))
+        cpool = ctx.enter_context(tc.tile_pool(name="cpool", bufs=10))
         opool = ctx.enter_context(tc.tile_pool(name="opool", bufs=NJB))
         pst = ctx.enter_context(tc.psum_pool(name="pst", bufs=8 - NI))
         psa = ctx.enter_context(tc.psum_pool(name="psa", bufs=NI))
@@ -260,14 +261,15 @@ def tile_testmmrsmodel_t_kernel(tc, hidden_states, gate_proj, world_size, out_0,
                     epilogue_stage(e[0], e[1], False)
                     e[1] += 1
                 pending = [e for e in pending if e[1] < 5]
-            if j >= 1:
-                for k in runs[j - 1]:
+            if j >= MM_LAG:
+                for k in runs[j - MM_LAG]:
                     matmuls(k)
                     if units[k][1] == R - 1:
                         epilogue_stage(units[k][0], 0, False)
                         pending.append([units[k][0], 1])
-        for k in runs[-1]:
-            matmuls(k)
+        for run in runs[len(runs) - MM_LAG :]:
+            for k in run:
+                matmuls(k)
         for e in pending:
             for stage in range(e[1], 5):
                 epilogue_stage(e[0], stage, False)

@@ -47,7 +47,7 @@ def unit_plan():
                     units.append((jb, r, i0, 2, False))
             else:
                 runs[-1].append(len(units))
-                units.append((jb, r, 0, NI, r % 2 == 1 and (jb, r) != (0, 1)))
+                units.append((jb, r, 0, NI, r % 4 != 0 and (jb, r) != (0, 1)))
     return units, runs
 
 

@@ -24,14 +24,19 @@ FP8_MAX = 448.0
 RUN = 8
 PRE_LEAD = 3
 MM_LAG = 2
+HALF = 2
+
+
+def is_split(jb, r):
+    return (jb, r) in ((0, 0), (NJB - 1, R - 1))
 
 
 def load_pieces(jb):
     if jb == 0:
-        return [1, 1, 2, 2, 2]
+        return [(0, 1, 0, HALF), (0, 1, HALF, HALF)] + [(r, 1, 0, NI) for r in range(1, R)]
     if jb == NJB - 1:
-        return [2, 2, 2, 1, 1]
-    return [2, 2, 2, 2]
+        return [(0, 2, 0, NI), (2, 2, 0, NI), (4, 2, 0, NI), (6, 1, 0, NI), (7, 1, 0, NI)]
+    return [(r, 2, 0, NI) for r in range(0, R, 2)]
 
 
 def unit_plan():
@@ -41,13 +46,13 @@ def unit_plan():
         for r in range(R):
             if r % 2 == 0:
                 runs.append([])
-            if jb == NJB - 1 and r == R - 1:
-                for i0 in range(0, NI, 2):
+            if is_split(jb, r):
+                for i0 in range(0, NI, HALF):
                     runs[-1].append(len(units))
-                    units.append((jb, r, i0, 2, False))
+                    units.append((jb, r, i0, HALF, False))
             else:
                 runs[-1].append(len(units))
-                units.append((jb, r, 0, NI, r % 4 != 0 and (jb, r) != (0, 1)))
+                units.append((jb, r, 0, NI, r % 4 != 0 and (jb, r) > (0, 2)))
     return units, runs
 
 
@@ -74,21 +79,28 @@ def tile_testmmrsmodel_t_kernel(tc, hidden_states, gate_proj, world_size, out_0,
 
         where = {}
         gate_sb = keep.tile([P, K], BF16, name="gate_sb")
+        all_rows = hidden_states.flatten_outer_dims()
         for jb in range(NJB):
-            r0 = 0
-            for nr in load_pieces(jb):
-                x = keep.tile([P, nr * NI * K], BF16, name="x%d_%d" % (jb, r0))
-                nc.sync.dma_start(
-                    out=x[:].rearrange("p (r e) -> p r e", r=nr),
-                    in_=hidden_states[r0 : r0 + nr, jb * P * NI : (jb + 1) * P * NI, :].rearrange(
-                        "r (p i) k -> p r (i k)", i=NI
-                    ),
-                )
+            for r0, nr, i0, ni in load_pieces(jb):
+                x = keep.tile([P, nr * ni * K], BF16, name="x%d_%d_%d" % (jb, r0, i0))
+                if ni == NI:
+                    nc.sync.dma_start(
+                        out=x[:].rearrange("p (r e) -> p r e", r=nr),
+                        in_=hidden_states[r0 : r0 + nr, jb * P * NI : (jb + 1) * P * NI, :].rearrange(
+                            "r (p i) k -> p r (i k)", i=NI
+                        ),
+                    )
+                else:
+                    row0 = r0 * J + jb * P * NI
+                    nc.sync.dma_start(
+                        out=x[:].rearrange("p (i k) -> p i k", i=ni),
+                        in_=all_rows[row0 : row0 + P * NI, :].rearrange("(p i) k -> p i k", i=NI)[:, i0 : i0 + ni, :],
+                    )
                 for rr in range(nr):
-                    where[(jb, r0 + rr)] = (x[:].bitcast(F32), rr * NI * KW)
-                if jb == 0 and r0 == 0:
+                    for i in range(ni):
+                        where[(jb, r0 + rr, i0 + i)] = (x[:].bitcast(F32), (rr * ni + i) * KW)
+                if (jb, r0, i0) == (0, 0, 0):
                     nc.sync.dma_start(out=gate_sb[:], in_=gate_proj[:, :])
-                r0 += nr
 
         units, runs = unit_plan()
         pcs = {}
@@ -109,9 +121,9 @@ def tile_testmmrsmodel_t_kernel(tc, hidden_states, gate_proj, world_size, out_0,
             if k >= len(units) or not units[k][4]:
                 return
             jb, r, i0, ni, pre = units[k]
-            words, off = where[(jb, r)]
+            words, off = where[(jb, r, i0)]
             pc = ppool.tile([P, 2, ni * KW // 2], F32, name="pc")
-            deinterleave_words(pc[:], words[:, off + i0 * KW : off + (i0 + ni) * KW])
+            deinterleave_words(pc[:], words[:, off : off + ni * KW])
             pcs[k] = pc
 
         def transpose_pair(xt, a, src):
@@ -129,8 +141,7 @@ def tile_testmmrsmodel_t_kernel(tc, hidden_states, gate_proj, world_size, out_0,
                         pc = pcs[k]
                         transpose_pair(xt, a, lambda u: pc[:, u, t * P : (t + 1) * P])
                     else:
-                        words, off = where[(jb, r)]
-                        lo = off + (i0 + t) * KW
+                        words, lo = where[(jb, r, i0 + t)]
                         transpose_pair(xt, a, lambda u: words[:, lo + u : lo + KW : 2])
                 banks[k].append(xt)
 
@@ -140,20 +151,12 @@ def tile_testmmrsmodel_t_kernel(tc, hidden_states, gate_proj, world_size, out_0,
                 in_=xt[:, 0:n, :, :].rearrange("p a u r -> p a r u"),
             )
 
-        late_stores = []
-
         def drains_and_quantize(k):
             jb, r, i0, ni, pre = units[k]
             g = gpool.tile([P, ni * K], BF16, name="g", align_bytes=64)
             gw = g[:].bitcast(F32)
             for b in range(ni // 2):
                 drain(banks[k][b], 2, gw[:, 2 * b * KW : 2 * (b + 1) * KW])
-            if k == len(units) - 2:
-                for rows, o32 in late_stores:
-                    nc.scalar.dma_start(
-                        out=out_0[rows, :].rearrange("(p i) o -> p (i o)", i=NI),
-                        in_=o32[:].rearrange("p i o -> p (i o)"),
-                    )
             codes = cpool.tile([P, ni * P], U32, name="codes", align_bytes=64)
             scl = cpool.tile([P, ni * P], U8, name="scl", align_bytes=64)
             nc.vector.quantize_mx(out=codes[:].bitcast(FP8X4), scales=scl[:], in_=g[:])
@@ -180,62 +183,86 @@ def tile_testmmrsmodel_t_kernel(tc, hidden_states, gate_proj, world_size, out_0,
 
         ep = {}
 
-        def epilogue_stage(jb, stage, last):
-            rows = slice(jb * P * NI, (jb + 1) * P * NI)
-            if stage == 0:
-                o32 = opool.tile([P, NI, O], F32, name="o32")
-                for i in range(NI):
-                    if last and i == NI - 1:
-                        nc.vector.tensor_copy(out=o32[:, i, :], in_=acc[i][:])
-                    else:
-                        nc.scalar.copy(out=o32[:, i, :], in_=acc[i][:])
-                if last:
-                    nc.sync.dma_start(
-                        out=out_0[rows, :].rearrange("(p i) o -> p (i o)", i=NI),
-                        in_=o32[:].rearrange("p i o -> p (i o)"),
-                    )
-                else:
-                    late_stores.append((rows, o32))
-                ep[jb] = {"o32": o32}
-            elif stage == 1:
-                amax = opool.tile([P, NI], F32, name="amax")
-                nc.vector.tensor_reduce(
-                    out=amax[:], in_=ep[jb]["o32"][:], axis=AX.X, op=ALU.max, apply_absolute_value=True
+        def rows_of(jb):
+            return slice(jb * P * NI, (jb + 1) * P * NI)
+
+        def open_epilogue(jb):
+            ep[jb] = {
+                "o32": opool.tile([P, NI, O], F32, name="o32"),
+                "amax": opool.tile([P, NI], F32, name="amax"),
+                "rc": opool.tile([P, NI], F32, name="rc"),
+                "rs": opool.tile([P, NI], F32, name="rs"),
+                "o8": opool.tile([P, NI, O], FP8, name="o8"),
+            }
+
+        def copy_sums(jb, i_lo, i_hi):
+            for i in range(i_lo, i_hi):
+                nc.scalar.copy(out=ep[jb]["o32"][:, i, :], in_=acc[i][:])
+
+        def store_sums(jb):
+            nc.sync.dma_start(
+                out=out_0[rows_of(jb), :].rearrange("(p i) o -> p (i o)", i=NI),
+                in_=ep[jb]["o32"][:].rearrange("p i o -> p (i o)"),
+            )
+
+        def row_maxima(jb, i_lo, i_hi):
+            nc.vector.tensor_reduce(
+                out=ep[jb]["amax"][:, i_lo:i_hi],
+                in_=ep[jb]["o32"][:, i_lo:i_hi, :],
+                axis=AX.X,
+                op=ALU.max,
+                apply_absolute_value=True,
+            )
+
+        def reciprocals(jb, i_lo, i_hi):
+            nc.vector.reciprocal(out=ep[jb]["rc"][:, i_lo:i_hi], in_=ep[jb]["amax"][:, i_lo:i_hi])
+
+        def factors(jb, i_lo, i_hi):
+            nc.vector.tensor_scalar(
+                out=ep[jb]["rs"][:, i_lo:i_hi], in0=ep[jb]["rc"][:, i_lo:i_hi], scalar1=FP8_MAX, scalar2=None, op0=ALU.mult
+            )
+
+        def cast(jb, i, on_scalar):
+            if on_scalar:
+                nc.scalar.activation(
+                    out=ep[jb]["o8"][:, i, :],
+                    in_=ep[jb]["o32"][:, i, :],
+                    func=ACT.Identity,
+                    scale=ep[jb]["rs"][:, i : i + 1],
+                    bias=zero[:, 0:1],
+                    saturate=False,
                 )
-                ep[jb]["amax"] = amax
-            elif stage == 2:
-                rc = opool.tile([P, NI], F32, name="rc")
-                nc.vector.reciprocal(out=rc[:], in_=ep[jb]["amax"][:])
-                ep[jb]["rc"] = rc
-            elif stage == 3:
-                rs = opool.tile([P, NI], F32, name="rs")
-                nc.vector.tensor_scalar(out=rs[:], in0=ep[jb]["rc"][:], scalar1=FP8_MAX, scalar2=None, op0=ALU.mult)
-                ep[jb]["rs"] = rs
             else:
-                o8 = opool.tile([P, NI, O], FP8, name="o8")
-                for i in range(NI):
-                    if last and i % 2 == 1:
-                        nc.scalar.activation(
-                            out=o8[:, i, :],
-                            in_=ep[jb]["o32"][:, i, :],
-                            func=ACT.Identity,
-                            scale=ep[jb]["rs"][:, i : i + 1],
-                            bias=zero[:, 0:1],
-                            saturate=False,
-                        )
-                    else:
-                        nc.vector.tensor_scalar(
-                            out=o8[:, i, :],
-                            in0=ep[jb]["o32"][:, i, :],
-                            scalar1=ep[jb]["rs"][:, i : i + 1],
-                            scalar2=None,
-                            op0=ALU.mult,
-                            saturate=False,
-                        )
-                nc.sync.dma_start(
-                    out=out_1[rows, :].rearrange("(p i) o -> p (i o)", i=NI),
-                    in_=o8[:].rearrange("p i o -> p (i o)").bitcast(U8),
+                nc.vector.tensor_scalar(
+                    out=ep[jb]["o8"][:, i, :],
+                    in0=ep[jb]["o32"][:, i, :],
+                    scalar1=ep[jb]["rs"][:, i : i + 1],
+                    scalar2=None,
+                    op0=ALU.mult,
+                    saturate=False,
                 )
+
+        def store_bytes(jb):
+            nc.sync.dma_start(
+                out=out_1[rows_of(jb), :].rearrange("(p i) o -> p (i o)", i=NI),
+                in_=ep[jb]["o8"][:].rearrange("p i o -> p (i o)").bitcast(U8),
+            )
+
+        def epilogue_stage(jb, stage):
+            if stage == 0:
+                open_epilogue(jb)
+                copy_sums(jb, 0, NI)
+                store_sums(jb)
+            elif stage == 1:
+                row_maxima(jb, 0, NI)
+            elif stage == 2:
+                reciprocals(jb, 0, NI)
+            elif stage == 3:
+                factors(jb, 0, NI)
+            else:
+                for i in range(NI):
+                    cast(jb, i, False)
+                store_bytes(jb)
 
         gpc = keep.tile([P, 2, KW // 2], F32, name="gpc")
         deinterleave_words(gpc[:], gate_sb[:].bitcast(F32))
@@ -257,21 +284,33 @@ def tile_testmmrsmodel_t_kernel(tc, hidden_states, gate_proj, world_size, out_0,
                     drain(gxt, 2, gg[:].bitcast(F32))
                 if k == 1:
                     nc.vector.quantize_mx(out=gcodes[:].bitcast(FP8X4), scales=gscl[:], in_=gg[:])
-                for e in pending:
-                    epilogue_stage(e[0], e[1], False)
-                    e[1] += 1
-                pending = [e for e in pending if e[1] < 5]
+                if j < len(runs) - 1:
+                    for e in pending:
+                        epilogue_stage(e[0], e[1])
+                        e[1] += 1
+                    pending = [e for e in pending if e[1] < 5]
             if j >= MM_LAG:
                 for k in runs[j - MM_LAG]:
                     matmuls(k)
                     if units[k][1] == R - 1:
-                        epilogue_stage(units[k][0], 0, False)
+                        epilogue_stage(units[k][0], 0)
                         pending.append([units[k][0], 1])
+        for e in pending:
+            for stage in range(e[1], 5):
+                epilogue_stage(e[0], stage)
+
+        last = NJB - 1
+        open_epilogue(last)
         for run in runs[len(runs) - MM_LAG :]:
             for k in run:
                 matmuls(k)
-        for e in pending:
-            for stage in range(e[1], 5):
-                epilogue_stage(e[0], stage, False)
-        for stage in range(5):
-            epilogue_stage(NJB - 1, stage, True)
+                if units[k][1] == R - 1:
+                    copy_sums(last, units[k][2], units[k][2] + units[k][3])
+        store_sums(last)
+        for i_lo in range(0, NI, HALF):
+            row_maxima(last, i_lo, i_lo + HALF)
+        reciprocals(last, 0, NI)
+        factors(last, 0, NI)
+        for i in range(NI):
+            cast(last, i, i % 2 == 1)
+        store_bytes(last)

@@ -23,17 +23,47 @@ NJB = J // (P * NI)
 FP8_MAX = 448.0
 RUN = 8
 PRE_LEAD = 3
-MM_LAG = 2
+N_OPEN = 4
+OPEN_LAG = 2
+MM_AFTER_2 = 4
+MM_AFTER = 4
+MM_PARTS = 1
+MM_STEP = 2
+SUMS_AFTER = 1
+FINE_TO = 3
+WIDE = 0
+WIDE_TO = 3
+G_BUFS = 4
+C_BUFS = 10
+V_RS = (4,)
+PRE_RS = (1,2,3,5,6,7)
+PRE_FROM = 2
+V_FROM = 3
+GATE_LOAD = 5
+GATE_COPY = 2
+GATE_UNIT = 7
 HALF = 2
+FIRST_SPLIT = ((0,2),(2,2))
+LAST_SPLIT = ((0,2),(2,2))
+HOLD = 3
+N_SCALAR_CASTS = 2
+GATE_K = 0
+GATE_AT = 0
 
 
-def is_split(jb, r):
-    return (jb, r) in ((0, 0), (NJB - 1, R - 1))
+def splits(jb, r):
+    if (jb, r) == (0, 0):
+        return FIRST_SPLIT
+    if (jb, r) == (NJB - 1, R - 1):
+        return LAST_SPLIT
+    return ((0, NI),)
 
 
 def load_pieces(jb):
     if jb == 0:
-        return [(0, 1, 0, HALF), (0, 1, HALF, HALF)] + [(r, 1, 0, NI) for r in range(1, R)]
+        return [(0, 1, i0, ni) for i0, ni in FIRST_SPLIT] + [(r, 1, 0, NI) for r in range(1, R)]
+    if jb < FINE_TO:
+        return [(r, 1, 0, NI) for r in range(R)]
     if jb == NJB - 1:
         return [(0, 2, 0, NI), (2, 2, 0, NI), (4, 2, 0, NI), (6, 1, 0, NI), (7, 1, 0, NI)]
     return [(r, 2, 0, NI) for r in range(0, R, 2)]
@@ -41,19 +71,11 @@ def load_pieces(jb):
 
 def unit_plan():
     units = []
-    runs = []
     for jb in range(NJB):
         for r in range(R):
-            if r % 2 == 0:
-                runs.append([])
-            if is_split(jb, r):
-                for i0 in range(0, NI, HALF):
-                    runs[-1].append(len(units))
-                    units.append((jb, r, i0, HALF, False))
-            else:
-                runs[-1].append(len(units))
-                units.append((jb, r, 0, NI, r % 4 != 0 and (jb, r) > (0, 2)))
-    return units, runs
+            for i0, ni in splits(jb, r):
+                units.append((jb, r, i0, ni, ni == NI and r in PRE_RS and (jb, r) > (0, PRE_FROM)))
+    return units, None
 
 
 def tile_testmmrsmodel_t_kernel(tc, hidden_states, gate_proj, world_size, out_0, out_1):
@@ -63,11 +85,10 @@ def tile_testmmrsmodel_t_kernel(tc, hidden_states, gate_proj, world_size, out_0,
     with ExitStack() as ctx:
         keep = ctx.enter_context(tc.tile_pool(name="keep", bufs=1))
         ppool = ctx.enter_context(tc.tile_pool(name="ppool", bufs=PRE_LEAD + 1))
-        gpool = ctx.enter_context(tc.tile_pool(name="gpool", bufs=4))
-        cpool = ctx.enter_context(tc.tile_pool(name="cpool", bufs=10))
+        gpool = ctx.enter_context(tc.tile_pool(name="gpool", bufs=G_BUFS))
+        cpool = ctx.enter_context(tc.tile_pool(name="cpool", bufs=C_BUFS))
         opool = ctx.enter_context(tc.tile_pool(name="opool", bufs=NJB))
-        pst = ctx.enter_context(tc.psum_pool(name="pst", bufs=8 - NI))
-        psa = ctx.enter_context(tc.psum_pool(name="psa", bufs=NI))
+        psum = ctx.enter_context(tc.psum_pool(name="psum", bufs=8))
         ctx.enter_context(tc.manual_schedule())
 
         ident = keep.tile([P, P], F32, name="ident")
@@ -80,6 +101,7 @@ def tile_testmmrsmodel_t_kernel(tc, hidden_states, gate_proj, world_size, out_0,
         where = {}
         gate_sb = keep.tile([P, K], BF16, name="gate_sb")
         all_rows = hidden_states.flatten_outer_dims()
+        n_loads = []
         for jb in range(NJB):
             for r0, nr, i0, ni in load_pieces(jb):
                 x = keep.tile([P, nr * ni * K], BF16, name="x%d_%d_%d" % (jb, r0, i0))
@@ -99,7 +121,8 @@ def tile_testmmrsmodel_t_kernel(tc, hidden_states, gate_proj, world_size, out_0,
                 for rr in range(nr):
                     for i in range(ni):
                         where[(jb, r0 + rr, i0 + i)] = (x[:].bitcast(F32), (rr * ni + i) * KW)
-                if (jb, r0, i0) == (0, 0, 0):
+                n_loads.append(1)
+                if len(n_loads) == GATE_AT + 1:
                     nc.sync.dma_start(out=gate_sb[:], in_=gate_proj[:, :])
 
         units, runs = unit_plan()
@@ -107,6 +130,8 @@ def tile_testmmrsmodel_t_kernel(tc, hidden_states, gate_proj, world_size, out_0,
         banks = {}
         quant = {}
         acc = {}
+        sums = {}
+        gs = {}
         gcodes = keep.tile([P, 2 * O], U32, name="gcodes", align_bytes=64)
         gscl = keep.tile([P, 2 * O], U8, name="gscl", align_bytes=64)
         gg = keep.tile([P, 2 * K], BF16, name="gg", align_bytes=64)
@@ -133,9 +158,9 @@ def tile_testmmrsmodel_t_kernel(tc, hidden_states, gate_proj, world_size, out_0,
         def transposes(k):
             jb, r, i0, ni, pre = units[k]
             banks[k] = []
-            for b in range(ni // 2):
-                xt = pst.tile([P, 2, 2, P], F32, name="xt")
-                for a in range(2):
+            for b in range((ni + 1) // 2):
+                xt = psum.tile([P, 2, 2, P], F32, name="bank")
+                for a in range(min(2, ni - 2 * b)):
                     t = 2 * b + a
                     if pre:
                         pc = pcs[k]
@@ -151,35 +176,85 @@ def tile_testmmrsmodel_t_kernel(tc, hidden_states, gate_proj, world_size, out_0,
                 in_=xt[:, 0:n, :, :].rearrange("p a u r -> p a r u"),
             )
 
-        def drains_and_quantize(k):
+        def wide(k):
             jb, r, i0, ni, pre = units[k]
-            g = gpool.tile([P, ni * K], BF16, name="g", align_bytes=64)
-            gw = g[:].bitcast(F32)
-            for b in range(ni // 2):
-                drain(banks[k][b], 2, gw[:, 2 * b * KW : 2 * (b + 1) * KW])
-            codes = cpool.tile([P, ni * P], U32, name="codes", align_bytes=64)
-            scl = cpool.tile([P, ni * P], U8, name="scl", align_bytes=64)
-            nc.vector.quantize_mx(out=codes[:].bitcast(FP8X4), scales=scl[:], in_=g[:])
-            quant[k] = (codes, scl)
+            return WIDE and N_OPEN <= jb < WIDE_TO
 
-        def matmuls(k):
+        def vector_drains(k):
             jb, r, i0, ni, pre = units[k]
-            codes, scl = quant[k]
+            return ni == NI and (jb, r) >= (V_FROM, 0) and r in V_RS
+
+        def drains(k):
+            jb, r, i0, ni, pre = units[k]
+            if wide(k) and r % 2 == 1:
+                g = gs[k - 1]
+                base = NI * KW
+            else:
+                g = gpool.tile([P, (2 if wide(k) else 1) * ni * K], BF16, name="g", align_bytes=64)
+                base = 0
+            gs[k] = g
+            gw = g[:].bitcast(F32)
+            for b in range((ni + 1) // 2):
+                n = min(2, ni - 2 * b)
+                dst = gw[:, base + 2 * b * KW : base + (2 * b + n) * KW]
+                if b == 1 and vector_drains(k):
+                    nc.vector.tensor_copy(
+                        out=dst.rearrange("p (a r u) -> p a r u", a=2, u=2),
+                        in_=banks[k][b][:, :, :, :].rearrange("p a u r -> p a r u"),
+                    )
+                else:
+                    drain(banks[k][b], n, dst)
+
+        def quantize(k):
+            jb, r, i0, ni, pre = units[k]
+            g = gs[k]
+            if wide(k) and r % 2 == 0:
+                return
+            n = 2 if wide(k) else 1
+            codes = cpool.tile([P, n * ni * P], U32, name="codes", align_bytes=64)
+            scl = cpool.tile([P, n * ni * P], U8, name="scl", align_bytes=64)
+            nc.vector.quantize_mx(out=codes[:].bitcast(FP8X4), scales=scl[:], in_=g[:])
+            quant[k] = (codes, scl, (n - 1) * ni * P)
+            if wide(k):
+                quant[k - 1] = (codes, scl, 0)
+
+        def one_pass(k, i, out, start, stop):
+            jb, r, i0, ni, pre = units[k]
+            codes, scl, c0 = quant[k]
             gcols = slice(O, 2 * O) if pre else slice(0, O)
-            for t in range(ni):
-                i = i0 + t
+            cols = slice(c0 + (i - i0) * P, c0 + (i - i0 + 1) * P)
+            nc.tensor.matmul_mx(
+                out=out,
+                lhsT=codes[:, cols].bitcast(FP8X4),
+                lhsT_scale=scl[:, cols],
+                rhs=gcodes[:, gcols].bitcast(FP8X4),
+                rhs_scale=gscl[:, gcols],
+                start=start,
+                stop=stop,
+            )
+
+        def units_of(jb, i):
+            return [k for k in range(len(units)) if units[k][0] == jb and units[k][2] <= i < units[k][2] + units[k][3]]
+
+        def unit_passes(k):
+            jb, r, i0, ni, pre = units[k]
+            for i in range(i0, i0 + ni):
                 if r == 0:
-                    acc[i] = psa.tile([P, O], F32, name="acc")
-                cols = slice(t * P, (t + 1) * P)
-                nc.tensor.matmul_mx(
-                    out=acc[i][:],
-                    lhsT=codes[:, cols].bitcast(FP8X4),
-                    lhsT_scale=scl[:, cols],
-                    rhs=gcodes[:, gcols].bitcast(FP8X4),
-                    rhs_scale=gscl[:, gcols],
-                    start=(r == 0),
-                    stop=(r == R - 1),
-                )
+                    acc[i] = psum.tile([P, O], F32, name="bank")
+                one_pass(k, i, acc[i][:], r == 0, r == R - 1)
+
+        def chunk_passes(jb, r_lo, r_hi):
+            for k in range(len(units)):
+                if units[k][0] == jb and r_lo <= units[k][1] < r_hi:
+                    unit_passes(k)
+
+        def block_passes(jb, i_lo, i_hi):
+            if i_lo == 0:
+                sums[jb] = psum.tile([P, NI, O], F32, name="bank")
+            for i in range(i_lo, i_hi):
+                ks = units_of(jb, i)
+                for n, k in enumerate(ks):
+                    one_pass(k, i, sums[jb][:, i, :], n == 0, n == len(ks) - 1)
 
         ep = {}
 
@@ -198,6 +273,9 @@ def tile_testmmrsmodel_t_kernel(tc, hidden_states, gate_proj, world_size, out_0,
         def copy_sums(jb, i_lo, i_hi):
             for i in range(i_lo, i_hi):
                 nc.scalar.copy(out=ep[jb]["o32"][:, i, :], in_=acc[i][:])
+
+        def copy_block_sums(jb):
+            nc.scalar.copy(out=ep[jb]["o32"][:], in_=sums[jb][:])
 
         def store_sums(jb):
             nc.sync.dma_start(
@@ -251,7 +329,10 @@ def tile_testmmrsmodel_t_kernel(tc, hidden_states, gate_proj, world_size, out_0,
         def epilogue_stage(jb, stage):
             if stage == 0:
                 open_epilogue(jb)
-                copy_sums(jb, 0, NI)
+                if jb < N_OPEN:
+                    copy_sums(jb, 0, NI)
+                else:
+                    copy_block_sums(jb)
                 store_sums(jb)
             elif stage == 1:
                 row_maxima(jb, 0, NI)
@@ -269,48 +350,80 @@ def tile_testmmrsmodel_t_kernel(tc, hidden_states, gate_proj, world_size, out_0,
         for k in range(PRE_LEAD):
             deinterleave(k)
 
-        pending = []
-        for j, run in enumerate(runs):
-            for k in run:
-                deinterleave(k + PRE_LEAD)
-                transposes(k)
-                if k == 0:
-                    gxt = pst.tile([P, 2, 2, P], F32, name="xt")
-                    gwords = gate_sb[:].bitcast(F32)
-                    transpose_pair(gxt, 0, lambda u: gwords[:, u:KW:2])
-                    transpose_pair(gxt, 1, lambda u: gpc[:, u, :])
-                drains_and_quantize(k)
-                if k == 0:
-                    drain(gxt, 2, gg[:].bitcast(F32))
-                if k == 1:
-                    nc.vector.quantize_mx(out=gcodes[:].bitcast(FP8X4), scales=gscl[:], in_=gg[:])
-                if j < len(runs) - 1:
-                    for e in pending:
-                        epilogue_stage(e[0], e[1])
-                        e[1] += 1
-                    pending = [e for e in pending if e[1] < 5]
-            if j >= MM_LAG:
-                for k in runs[j - MM_LAG]:
-                    matmuls(k)
-                    if units[k][1] == R - 1:
-                        epilogue_stage(units[k][0], 0)
-                        pending.append([units[k][0], 1])
-        for e in pending:
-            for stage in range(e[1], 5):
-                epilogue_stage(e[0], stage)
-
         last = NJB - 1
+        todo = {}
+
+        def last_unit(jb, r):
+            return [k for k in range(len(units)) if units[k][0:2] == (jb, r)][-1]
+
+        def chunk_after(jb, r, n):
+            c = jb * R + r + n
+            return last_unit(c // R, c % R)
+
+        early = []
+        if N_OPEN > last:
+            for r in range(1, R - 2 * OPEN_LAG, 2):
+                todo.setdefault(chunk_after(last, r, 2 * OPEN_LAG), []).append(("chunks", last, r - 1, r + 1))
+                early.extend([r - 1, r])
+        for jb in range(last):
+            if jb < N_OPEN:
+                for r in range(1, R, 2):
+                    at = chunk_after(jb, r, 2 * OPEN_LAG)
+                    todo.setdefault(at, []).append(("chunks", jb, r - 1, r + 1))
+                first_stage = at
+            else:
+                step = NI // MM_PARTS
+                after = MM_AFTER if jb < last - 1 else MM_AFTER_2
+                for part in range(MM_PARTS):
+                    at = chunk_after(jb, R - 1, after + part * MM_STEP)
+                    todo.setdefault(at, []).append(("passes", jb, part * step, (part + 1) * step))
+                first_stage = at + SUMS_AFTER
+            for stage in range(5):
+                todo.setdefault(first_stage + stage, []).append(("stage", jb, stage))
+
+        held = []
+        for k in range(len(units)):
+            transposes(k)
+            if k == GATE_K:
+                gxt = psum.tile([P, 2, 2, P], F32, name="bank")
+                gwords = gate_sb[:].bitcast(F32)
+                transpose_pair(gxt, 0, lambda u: gwords[:, u:KW:2])
+                transpose_pair(gxt, 1, lambda u: gpc[:, u, :])
+            drains(k)
+            deinterleave(k + PRE_LEAD)
+            quantize(k)
+            if k == GATE_K:
+                drain(gxt, 2, gg[:].bitcast(F32))
+            if k == GATE_K + 1:
+                nc.vector.quantize_mx(out=gcodes[:].bitcast(FP8X4), scales=gscl[:], in_=gg[:])
+            for job in todo.get(k, []):
+                if job[0] == "stage" and k >= len(units) - HOLD:
+                    held.append(job)
+                elif job[0] == "passes":
+                    block_passes(job[1], job[2], job[3])
+                elif job[0] == "chunks":
+                    chunk_passes(job[1], job[2], job[3])
+                else:
+                    epilogue_stage(job[1], job[2])
+        for k in sorted(todo):
+            if k >= len(units):
+                held.extend(todo[k])
+        for job in held:
+            assert job[0] == "stage"
+            epilogue_stage(job[1], job[2])
+
         open_epilogue(last)
-        for run in runs[len(runs) - MM_LAG :]:
-            for k in run:
-                matmuls(k)
-                if units[k][1] == R - 1:
-                    copy_sums(last, units[k][2], units[k][2] + units[k][3])
+        for k in range(len(units)):
+            jb, r, i0, ni, pre = units[k]
+            if jb == last and r not in early:
+                unit_passes(k)
+                if r == R - 1:
+                    copy_sums(last, i0, i0 + ni)
         store_sums(last)
-        for i_lo in range(0, NI, HALF):
-            row_maxima(last, i_lo, i_lo + HALF)
+        for i_lo, ni in LAST_SPLIT:
+            row_maxima(last, i_lo, i_lo + ni)
         reciprocals(last, 0, NI)
         factors(last, 0, NI)
         for i in range(NI):
-            cast(last, i, i % 2 == 1)
+            cast(last, i, i >= NI - N_SCALAR_CASTS)
         store_bytes(last)

from contextlib import ExitStack

import concourse.mybir as mybir
from concourse.masks import make_identity

F32 = mybir.dt.float32
BF16 = mybir.dt.bfloat16
U32 = mybir.dt.uint32
U8 = mybir.dt.uint8
FP8X4 = mybir.dt.float8_e4m3fn_x4
FP8 = mybir.dt.float8_e4m3fn
ALU = mybir.AluOpType
ACT = mybir.ActivationFunctionType
AX = mybir.AxisListType

R, J, K, O = 8, 2048, 512, 128
FLOPS = 2 * R * J * K * O

P = 128
KW = K // 2
NI = 4
NJB = J // (P * NI)
FP8_MAX = 448.0
RUN = 8
PRE_LEAD = 3
N_OPEN = 4
OPEN_LAG = 2
MM_AFTER_2 = 4
MM_AFTER = 4
MM_PARTS = 1
MM_STEP = 2
SUMS_AFTER = 1
FINE_TO = 3
WIDE = 0
WIDE_TO = 3
G_BUFS = 4
C_BUFS = 10
V_RS = (4,)
PRE_RS = (1,2,3,5,6,7)
PRE_FROM = 2
V_FROM = 3
GATE_LOAD = 5
GATE_COPY = 2
GATE_UNIT = 7
HALF = 2
FIRST_SPLIT = ((0,2),(2,2))
LAST_SPLIT = ((0,2),(2,2))
HOLD = 3
N_SCALAR_CASTS = 2
GATE_K = 0
GATE_AT = 0


def splits(jb, r):
    if (jb, r) == (0, 0):
        return FIRST_SPLIT
    if (jb, r) == (NJB - 1, R - 1):
        return LAST_SPLIT
    return ((0, NI),)


def load_pieces(jb):
    if jb == 0:
        return [(0, 1, i0, ni) for i0, ni in FIRST_SPLIT] + [(r, 1, 0, NI) for r in range(1, R)]
    if jb < FINE_TO:
        return [(r, 1, 0, NI) for r in range(R)]
    if jb == NJB - 1:
        return [(0, 2, 0, NI), (2, 2, 0, NI), (4, 2, 0, NI), (6, 1, 0, NI), (7, 1, 0, NI)]
    return [(r, 2, 0, NI) for r in range(0, R, 2)]


def unit_plan():
    units = []
    for jb in range(NJB):
        for r in range(R):
            for i0, ni in splits(jb, r):
                units.append((jb, r, i0, ni, ni == NI and r in PRE_RS and (jb, r) > (0, PRE_FROM)))
    return units, None


def tile_testmmrsmodel_t_kernel(tc, hidden_states, gate_proj, world_size, out_0, out_1):
    nc = tc.nc
    assert world_size == R

    with ExitStack() as ctx:
        keep = ctx.enter_context(tc.tile_pool(name="keep", bufs=1))
        ppool = ctx.enter_context(tc.tile_pool(name="ppool", bufs=PRE_LEAD + 1))
        gpool = ctx.enter_context(tc.tile_pool(name="gpool", bufs=G_BUFS))
        cpool = ctx.enter_context(tc.tile_pool(name="cpool", bufs=C_BUFS))
        opool = ctx.enter_context(tc.tile_pool(name="opool", bufs=NJB))
        psum = ctx.enter_context(tc.psum_pool(name="psum", bufs=8))
        ctx.enter_context(tc.manual_schedule())

        ident = keep.tile([P, P], F32, name="ident")
        make_identity(nc, ident[:])
        zero = keep.tile([P, 1], F32, name="zero")
        nc.gpsimd.memset(zero[:], 0.0)
        warm = keep.tile([P, 1], F32, name="warm")
        nc.scalar.activation(out=warm[:], in_=zero[:], func=ACT.Identity, scale=zero[:, 0:1], bias=zero[:, 0:1])

        where = {}
        gate_sb = keep.tile([P, K], BF16, name="gate_sb")
        all_rows = hidden_states.flatten_outer_dims()
        n_loads = []
        for jb in range(NJB):
            for r0, nr, i0, ni in load_pieces(jb):
                x = keep.tile([P, nr * ni * K], BF16, name="x%d_%d_%d" % (jb, r0, i0))
                if ni == NI:
                    nc.sync.dma_start(
                        out=x[:].rearrange("p (r e) -> p r e", r=nr),
                        in_=hidden_states[r0 : r0 + nr, jb * P * NI : (jb + 1) * P * NI, :].rearrange(
                            "r (p i) k -> p r (i k)", i=NI
                        ),
                    )
                else:
                    row0 = r0 * J + jb * P * NI
                    nc.sync.dma_start(
                        out=x[:].rearrange("p (i k) -> p i k", i=ni),
                        in_=all_rows[row0 : row0 + P * NI, :].rearrange("(p i) k -> p i k", i=NI)[:, i0 : i0 + ni, :],
                    )
                for rr in range(nr):
                    for i in range(ni):
                        where[(jb, r0 + rr, i0 + i)] = (x[:].bitcast(F32), (rr * ni + i) * KW)
                n_loads.append(1)
                if len(n_loads) == GATE_AT + 1:
                    nc.sync.dma_start(out=gate_sb[:], in_=gate_proj[:, :])

        units, runs = unit_plan()
        pcs = {}
        banks = {}
        quant = {}
        acc = {}
        sums = {}
        gs = {}
        gcodes = keep.tile([P, 2 * O], U32, name="gcodes", align_bytes=64)
        gscl = keep.tile([P, 2 * O], U8, name="gscl", align_bytes=64)
        gg = keep.tile([P, 2 * K], BF16, name="gg", align_bytes=64)

        def deinterleave_words(dst, src):
            nc.vector.tensor_copy(
                out=dst.rearrange("p u (b i) -> p u b i", i=RUN),
                in_=src.rearrange("p (b u i) -> p u b i", u=2, i=RUN),
            )

        def deinterleave(k):
            if k >= len(units) or not units[k][4]:
                return
            jb, r, i0, ni, pre = units[k]
            words, off = where[(jb, r, i0)]
            pc = ppool.tile([P, 2, ni * KW // 2], F32, name="pc")
            deinterleave_words(pc[:], words[:, off : off + ni * KW])
            pcs[k] = pc

        def transpose_pair(xt, a, src):
            for u in range(2):
                nc.tensor.transpose(xt[:, a, u, :], src(u), ident[:])

        def transposes(k):
            jb, r, i0, ni, pre = units[k]
            banks[k] = []
            for b in range((ni + 1) // 2):
                xt = psum.tile([P, 2, 2, P], F32, name="bank")
                for a in range(min(2, ni - 2 * b)):
                    t = 2 * b + a
                    if pre:
                        pc = pcs[k]
                        transpose_pair(xt, a, lambda u: pc[:, u, t * P : (t + 1) * P])
                    else:
                        words, lo = where[(jb, r, i0 + t)]
                        transpose_pair(xt, a, lambda u: words[:, lo + u : lo + KW : 2])
                banks[k].append(xt)

        def drain(xt, n, dst_words):
            nc.scalar.copy(
                out=dst_words.rearrange("p (a r u) -> p a r u", a=n, u=2),
                in_=xt[:, 0:n, :, :].rearrange("p a u r -> p a r u"),
            )

        def wide(k):
            jb, r, i0, ni, pre = units[k]
            return WIDE and N_OPEN <= jb < WIDE_TO

        def vector_drains(k):
            jb, r, i0, ni, pre = units[k]
            return ni == NI and (jb, r) >= (V_FROM, 0) and r in V_RS

        def drains(k):
            jb, r, i0, ni, pre = units[k]
            if wide(k) and r % 2 == 1:
                g = gs[k - 1]
                base = NI * KW
            else:
                g = gpool.tile([P, (2 if wide(k) else 1) * ni * K], BF16, name="g", align_bytes=64)
                base = 0
            gs[k] = g
            gw = g[:].bitcast(F32)
            for b in range((ni + 1) // 2):
                n = min(2, ni - 2 * b)
                dst = gw[:, base + 2 * b * KW : base + (2 * b + n) * KW]
                if b == 1 and vector_drains(k):
                    nc.vector.tensor_copy(
                        out=dst.rearrange("p (a r u) -> p a r u", a=2, u=2),
                        in_=banks[k][b][:, :, :, :].rearrange("p a u r -> p a r u"),
                    )
                else:
                    drain(banks[k][b], n, dst)

        def quantize(k):
            jb, r, i0, ni, pre = units[k]
            g = gs[k]
            if wide(k) and r % 2 == 0:
                return
            n = 2 if wide(k) else 1
            codes = cpool.tile([P, n * ni * P], U32, name="codes", align_bytes=64)
            scl = cpool.tile([P, n * ni * P], U8, name="scl", align_bytes=64)
            nc.vector.quantize_mx(out=codes[:].bitcast(FP8X4), scales=scl[:], in_=g[:])
            quant[k] = (codes, scl, (n - 1) * ni * P)
            if wide(k):
                quant[k - 1] = (codes, scl, 0)

        def one_pass(k, i, out, start, stop):
            jb, r, i0, ni, pre = units[k]
            codes, scl, c0 = quant[k]
            gcols = slice(O, 2 * O) if pre else slice(0, O)
            cols = slice(c0 + (i - i0) * P, c0 + (i - i0 + 1) * P)
            nc.tensor.matmul_mx(
                out=out,
                lhsT=codes[:, cols].bitcast(FP8X4),
                lhsT_scale=scl[:, cols],
                rhs=gcodes[:, gcols].bitcast(FP8X4),
                rhs_scale=gscl[:, gcols],
                start=start,
                stop=stop,
            )

        def units_of(jb, i):
            return [k for k in range(len(units)) if units[k][0] == jb and units[k][2] <= i < units[k][2] + units[k][3]]

        def unit_passes(k):
            jb, r, i0, ni, pre = units[k]
            for i in range(i0, i0 + ni):
                if r == 0:
                    acc[i] = psum.tile([P, O], F32, name="bank")
                one_pass(k, i, acc[i][:], r == 0, r == R - 1)

        def chunk_passes(jb, r_lo, r_hi):
            for k in range(len(units)):
                if units[k][0] == jb and r_lo <= units[k][1] < r_hi:
                    unit_passes(k)

        def block_passes(jb, i_lo, i_hi):
            if i_lo == 0:
                sums[jb] = psum.tile([P, NI, O], F32, name="bank")
            for i in range(i_lo, i_hi):
                ks = units_of(jb, i)
                for n, k in enumerate(ks):
                    one_pass(k, i, sums[jb][:, i, :], n == 0, n == len(ks) - 1)

        ep = {}

        def rows_of(jb):
            return slice(jb * P * NI, (jb + 1) * P * NI)

        def open_epilogue(jb):
            ep[jb] = {
                "o32": opool.tile([P, NI, O], F32, name="o32"),
                "amax": opool.tile([P, NI], F32, name="amax"),
                "rc": opool.tile([P, NI], F32, name="rc"),
                "rs": opool.tile([P, NI], F32, name="rs"),
                "o8": opool.tile([P, NI, O], FP8, name="o8"),
            }

        def copy_sums(jb, i_lo, i_hi):
            for i in range(i_lo, i_hi):
                nc.scalar.copy(out=ep[jb]["o32"][:, i, :], in_=acc[i][:])

        def copy_block_sums(jb):
            nc.scalar.copy(out=ep[jb]["o32"][:], in_=sums[jb][:])

        def store_sums(jb):
            nc.sync.dma_start(
                out=out_0[rows_of(jb), :].rearrange("(p i) o -> p (i o)", i=NI),
                in_=ep[jb]["o32"][:].rearrange("p i o -> p (i o)"),
            )

        def row_maxima(jb, i_lo, i_hi):
            nc.vector.tensor_reduce(
                out=ep[jb]["amax"][:, i_lo:i_hi],
                in_=ep[jb]["o32"][:, i_lo:i_hi, :],
                axis=AX.X,
                op=ALU.max,
                apply_absolute_value=True,
            )

        def reciprocals(jb, i_lo, i_hi):
            nc.vector.reciprocal(out=ep[jb]["rc"][:, i_lo:i_hi], in_=ep[jb]["amax"][:, i_lo:i_hi])

        def factors(jb, i_lo, i_hi):
            nc.vector.tensor_scalar(
                out=ep[jb]["rs"][:, i_lo:i_hi], in0=ep[jb]["rc"][:, i_lo:i_hi], scalar1=FP8_MAX, scalar2=None, op0=ALU.mult
            )

        def cast(jb, i, on_scalar):
            if on_scalar:
                nc.scalar.activation(
                    out=ep[jb]["o8"][:, i, :],
                    in_=ep[jb]["o32"][:, i, :],
                    func=ACT.Identity,
                    scale=ep[jb]["rs"][:, i : i + 1],
                    bias=zero[:, 0:1],
                    saturate=False,
                )
            else:
                nc.vector.tensor_scalar(
                    out=ep[jb]["o8"][:, i, :],
                    in0=ep[jb]["o32"][:, i, :],
                    scalar1=ep[jb]["rs"][:, i : i + 1],
                    scalar2=None,
                    op0=ALU.mult,
                    saturate=False,
                )

        def store_bytes(jb):
            nc.sync.dma_start(
                out=out_1[rows_of(jb), :].rearrange("(p i) o -> p (i o)", i=NI),
                in_=ep[jb]["o8"][:].rearrange("p i o -> p (i o)").bitcast(U8),
            )

        def epilogue_stage(jb, stage):
            if stage == 0:
                open_epilogue(jb)
                if jb < N_OPEN:
                    copy_sums(jb, 0, NI)
                else:
                    copy_block_sums(jb)
                store_sums(jb)
            elif stage == 1:
                row_maxima(jb, 0, NI)
            elif stage == 2:
                reciprocals(jb, 0, NI)
            elif stage == 3:
                factors(jb, 0, NI)
            else:
                for i in range(NI):
                    cast(jb, i, False)
                store_bytes(jb)

        gpc = keep.tile([P, 2, KW // 2], F32, name="gpc")
        deinterleave_words(gpc[:], gate_sb[:].bitcast(F32))
        for k in range(PRE_LEAD):
            deinterleave(k)

        last = NJB - 1
        todo = {}

        def last_unit(jb, r):
            return [k for k in range(len(units)) if units[k][0:2] == (jb, r)][-1]

        def chunk_after(jb, r, n):
            c = jb * R + r + n
            return last_unit(c // R, c % R)

        early = []
        if N_OPEN > last:
            for r in range(1, R - 2 * OPEN_LAG, 2):
                todo.setdefault(chunk_after(last, r, 2 * OPEN_LAG), []).append(("chunks", last, r - 1, r + 1))
                early.extend([r - 1, r])
        for jb in range(last):
            if jb < N_OPEN:
                for r in range(1, R, 2):
                    at = chunk_after(jb, r, 2 * OPEN_LAG)
                    todo.setdefault(at, []).append(("chunks", jb, r - 1, r + 1))
                first_stage = at
            else:
                step = NI // MM_PARTS
                after = MM_AFTER if jb < last - 1 else MM_AFTER_2
                for part in range(MM_PARTS):
                    at = chunk_after(jb, R - 1, after + part * MM_STEP)
                    todo.setdefault(at, []).append(("passes", jb, part * step, (part + 1) * step))
                first_stage = at + SUMS_AFTER
            for stage in range(5):
                todo.setdefault(first_stage + stage, []).append(("stage", jb, stage))

        held = []
        for k in range(len(units)):
            transposes(k)
            if k == GATE_K:
                gxt = psum.tile([P, 2, 2, P], F32, name="bank")
                gwords = gate_sb[:].bitcast(F32)
                transpose_pair(gxt, 0, lambda u: gwords[:, u:KW:2])
                transpose_pair(gxt, 1, lambda u: gpc[:, u, :])
            drains(k)
            deinterleave(k + PRE_LEAD)
            quantize(k)
            if k == GATE_K:
                drain(gxt, 2, gg[:].bitcast(F32))
            if k == GATE_K + 1:
                nc.vector.quantize_mx(out=gcodes[:].bitcast(FP8X4), scales=gscl[:], in_=gg[:])
            for job in todo.get(k, []):
                if job[0] == "stage" and k >= len(units) - HOLD:
                    held.append(job)
                elif job[0] == "passes":
                    block_passes(job[1], job[2], job[3])
                elif job[0] == "chunks":
                    chunk_passes(job[1], job[2], job[3])
                else:
                    epilogue_stage(job[1], job[2])
        for k in sorted(todo):
            if k >= len(units):
                held.extend(todo[k])
        for job in held:
            assert job[0] == "stage"
            epilogue_stage(job[1], job[2])

        open_epilogue(last)
        for k in range(len(units)):
            jb, r, i0, ni, pre = units[k]
            if jb == last and r not in early:
                unit_passes(k)
                if r == R - 1:
                    copy_sums(last, i0, i0 + ni)
        store_sums(last)
        for i_lo, ni in LAST_SPLIT:
            row_maxima(last, i_lo, i_lo + ni)
        reciprocals(last, 0, NI)
        factors(last, 0, NI)
        for i in range(NI):
            cast(last, i, i >= NI - N_SCALAR_CASTS)
        store_bytes(last)
